import numpy as np
import ml_dtypes


def mxq(x, axis, fmt="e4m3"):
    dtype, down = {"e4m3": (ml_dtypes.float8_e4m3fn, 7), "e5m2": (ml_dtypes.float8_e5m2, 14)}[fmt]
    v = np.moveaxis(np.asarray(x, np.float32).astype(ml_dtypes.bfloat16).astype(np.float64), axis, -1)
    blocks = v.reshape(v.shape[:-1] + (-1, 32))
    amax = np.abs(blocks).max(-1, keepdims=True)
    byte = np.maximum(np.where(amax > 0, np.frexp(amax)[1] - 1 + 127, 0) - down, 1)
    scale = np.exp2(byte - 127.0)
    codes = (blocks / scale).astype(np.float32).astype(dtype).astype(np.float64)
    return np.moveaxis((codes * scale).reshape(v.shape), -1, axis)


WIDE = False


def mx_kscale(k):
    if not WIDE:
        return np.ones(k)
    levels = np.array([10, -10, 5, -5, 0])
    a = np.random.permutation(np.resize(levels, k // 512 * 4)).reshape(k // 512, 4)
    idx = np.arange(k)
    return np.exp2(a[idx // 512, idx % 128 // 32])


BF16 = ml_dtypes.bfloat16


def bf(x):
    return np.asarray(x, np.float32).astype(BF16)


def f64(x):
    return np.asarray(x).astype(np.float64)


E2M1 = np.array([0.0, 0.5, 1.0, 1.5, 2.0, 3.0, 4.0, 6.0, -0.0, -0.5, -1.0, -1.5, -2.0, -3.0, -4.0, -6.0])


def pack_weight(w, fmt):
    k, n = w.shape
    w = f64(bf(w)).reshape(k // 32, 32, n)
    amax = np.abs(w).max(1)
    if fmt == "e4m3":
        byte = np.frexp(amax)[1] - 1 + 127 - 7
    else:
        mant, ex = np.frexp(amax / 6.0)
        byte = np.where(mant > 0.5, ex, ex - 1) + 127
    byte = np.clip(np.where(amax > 0, byte, 1), 1, 254)
    scaled = (w * np.exp2(127.0 - byte)[:, None, :]).reshape(k, n).astype(np.float32)
    by_word = np.ascontiguousarray(scaled.reshape(k // 512, 128, 4, n).transpose(0, 1, 3, 2))
    if fmt == "e4m3":
        words = by_word.astype(ml_dtypes.float8_e4m3fn).view(np.uint8)
    else:
        c = by_word.astype(ml_dtypes.float4_e2m1fn).view(np.uint8) & 0xF
        words = c[..., 0::2] | (c[..., 1::2] << 4)
    return np.ascontiguousarray(words), np.ascontiguousarray(byte.astype(np.uint8).reshape(k // 512, 16, n))


def unpack_weight(words, scales, fmt):
    g, p, n, _ = words.shape
    if fmt == "e4m3":
        vals = np.ascontiguousarray(words).view(ml_dtypes.float8_e4m3fn).astype(np.float64)
    else:
        nib = np.empty((g, p, n, 4), np.uint8)
        nib[..., 0::2] = words & 0xF
        nib[..., 1::2] = words >> 4
        vals = E2M1[nib]
    vals = vals * np.repeat(np.exp2(scales.astype(np.float64) - 127.0), 8, axis=1)[..., None]
    return vals.transpose(0, 1, 3, 2).reshape(g * 512, n)


B, N, C, D = 2, 512, 512, 512
ETA, TAU = 1.0, 1.5
FMT = "e4m3"


def setup_inputs():
    s, t = mx_kscale(C), mx_kscale(D)
    a = 2.0 * (C / D) ** 0.25 / np.sqrt(C)
    H_t = bf(np.random.standard_normal((B, N, C)) * s)
    A_stat = bf(np.random.random((N, N)))
    M_mask = bf(np.random.random((N, N)) - 0.25)
    Wq = np.random.standard_normal((D, C)) * a * t[:, None] / s
    Wk = np.random.standard_normal((D, C)) * a / t[:, None] / s
    Wq_words, Wq_scales = pack_weight(np.ascontiguousarray(Wq.T), FMT)
    Wk_words, Wk_scales = pack_weight(np.ascontiguousarray(Wk.T), FMT)
    return {"H_t": H_t,
            "A_stat": A_stat,
            "M_mask": M_mask,
            "Wq_words": Wq_words,
            "Wq_scales": Wq_scales,
            "Wk_words": Wk_words,
            "Wk_scales": Wk_scales}


def reference(H_t, A_stat, M_mask, Wq_words, Wq_scales, Wk_words, Wk_scales):
    c = H_t.shape[-1]
    hq = mxq(f64(H_t), 2, "e4m3")
    Q = hq @ unpack_weight(Wq_words, Wq_scales, FMT)
    K = hq @ unpack_weight(Wk_words, Wk_scales, FMT)
    logits = (mxq(Q, 2, "e4m3") @ mxq(K, 2, "e4m3").transpose(0, 2, 1)) / (np.sqrt(c) * TAU)
    logits = 0.5 * (logits + logits.transpose(0, 2, 1))
    n = logits.shape[-1]
    eye = np.eye(n, dtype=bool)
    logits = np.where(eye[None, :, :], -np.inf, logits)
    A_bias = np.where(eye, 0.0, f64(A_stat))
    logits = logits + ETA * A_bias[None, :, :]
    logits = np.where((f64(M_mask) <= 0)[None, :, :], -np.inf, logits)
    e = np.exp(logits - logits.max(-1, keepdims=True))
    return e / e.sum(-1, keepdims=True)

@@ -1,0 +1,193 @@
+import math
+from contextlib import ExitStack
+
+import concourse.mybir as mybir
+from concourse.masks import make_identity
+
+F32 = mybir.dt.float32
+BF16 = mybir.dt.bfloat16
+I32 = mybir.dt.int32
+U32 = mybir.dt.uint32
+U8 = mybir.dt.uint8
+FP8X4 = mybir.dt.float8_e4m3fn_x4
+ALU = mybir.AluOpType
+ACT = mybir.ActivationFunctionType
+AXIS = mybir.AxisListType
+
+P = 128
+PACK = 4
+B, N, C, D = 2, 512, 512, 512
+NODE_BLOCKS = N // P
+TAU = 1.5
+HALF_SCALE = 0.5 / (math.sqrt(C) * TAU)
+EXCLUDED = -1.0e30
+Q_SIDE, K_SIDE = 0, 1
+
+FLOPS = 2 * B * N * C * (2 * D) + 2 * B * N * N * D
+
+
+def tile_dynamicgraphattention_kernel(
+    tc, H_t, A_stat, M_mask, Wq_words, Wq_scales, Wk_words, Wk_scales, out
+):
+    nc = tc.nc
+    with ExitStack() as ctx:
+        keep = ctx.enter_context(tc.tile_pool(name="keep", bufs=1))
+        rows = ctx.enter_context(tc.tile_pool(name="rows", bufs=4))
+        stats = ctx.enter_context(tc.tile_pool(name="stats", bufs=4))
+        psum_flip = ctx.enter_context(tc.psum_pool(name="psum_flip", bufs=2))
+        psum_proj = ctx.enter_context(tc.psum_pool(name="psum_proj", bufs=4))
+        psum_score = ctx.enter_context(tc.psum_pool(name="psum_score", bufs=2))
+
+        identity = keep.tile([P, P], F32)
+        make_identity(nc, identity[:])
+        w_planes = keep.tile([P, 2, D], U8, align_bytes=64)
+        nc.vector.memset(w_planes[:].rearrange("p w n -> p (w n)").bitcast(I32), 0)
+        warm = keep.tile([P, 1], F32)
+        nc.vector.memset(warm[:], 0.0)
+        nc.scalar.activation(out=warm[:], in_=warm[:], func=ACT.Exp)
+
+        h_sb = keep.tile([P, B, NODE_BLOCKS, C], BF16)
+        w_words = keep.tile([P, 2, D], U32, align_bytes=64)
+        m_sb = keep.tile([P, NODE_BLOCKS, N], BF16)
+        a_sb = keep.tile([P, NODE_BLOCKS, N], BF16)
+
+        def load_h(b):
+            nc.sync.dma_start(out=h_sb[:, b], in_=H_t[b].rearrange("(j p) c -> p j c", p=P))
+
+        def load_scales(side, scales):
+            by_r = scales[0].rearrange("(Q r) n -> r Q n", r=4)
+            for r in range(4):
+                nc.sync.dma_start(
+                    out=w_planes[r:P:32, side, :].bitcast(I32), in_=by_r[r].bitcast(I32)
+                )
+
+        def load_words(side, words):
+            nc.sync.dma_start(
+                out=w_words[:, side, :].bitcast(I32),
+                in_=words[0].rearrange("p n t -> p (n t)").bitcast(I32),
+            )
+
+        load_h(0)
+        load_scales(Q_SIDE, Wq_scales)
+        load_h(1)
+        load_words(Q_SIDE, Wq_words)
+        load_words(K_SIDE, Wk_words)
+        load_scales(K_SIDE, Wk_scales)
+        nc.sync.dma_start(out=m_sb[:], in_=M_mask.rearrange("(j p) m -> p j m", p=P))
+        nc.sync.dma_start(out=a_sb[:], in_=A_stat.rearrange("(j p) m -> p j m", p=P))
+
+        h_pairs = keep.tile([P, B, N, 2], F32, align_bytes=64)
+        h_codes = keep.tile([P, B, N], U32, align_bytes=64)
+        h_plane = keep.tile([P, B, N], U8, align_bytes=64)
+
+        def flip_and_quantise_h(b):
+            for half in range(2):
+                flipped = psum_flip.tile([P, 2, 2 * P], F32)
+                for jj in range(2):
+                    words = h_sb[:, b, 2 * half + jj, :].bitcast(F32)
+                    for u in range(2):
+                        nc.tensor.transpose(
+                            flipped[:, u, jj * P : (jj + 1) * P], words[:, u : C // 2 : 2], identity[:]
+                        )
+                nodes = slice(2 * P * half, 2 * P * (half + 1))
+                copy = nc.vector.tensor_copy if half == 0 else nc.scalar.copy
+                copy(out=h_pairs[:, b, nodes, :], in_=flipped[:].rearrange("p u n -> p n u"))
+            nc.vector.quantize_mx(
+                out=h_codes[:, b, :].bitcast(FP8X4),
+                scales=h_plane[:, b, :],
+                in_=h_pairs[:, b].rearrange("p n u -> p (n u)").bitcast(BF16),
+            )
+
+        qk_grouped = keep.tile([P, B, 2, N, PACK], BF16, align_bytes=64)
+        qk_codes = keep.tile([P, B, 2, N], U32, align_bytes=64)
+        qk_planes = keep.tile([P, B, 2, N], U8, align_bytes=64)
+
+        def project(b, side, j, copy):
+            nodes = slice(j * P, (j + 1) * P)
+            acc = psum_proj.tile([P, PACK, P], F32)
+            for t in range(PACK):
+                features = slice(t * P, (t + 1) * P)
+                nc.tensor.matmul_mx(
+                    out=acc[:, t, :],
+                    lhsT=w_words[:, side, features].bitcast(FP8X4),
+                    lhsT_scale=w_planes[:, side, features],
+                    rhs=h_codes[:, b, nodes].bitcast(FP8X4),
+                    rhs_scale=h_plane[:, b, nodes],
+                    start=True,
+                    stop=True,
+                )
+            copy(out=qk_grouped[:, b, side, nodes, :], in_=acc[:].rearrange("p t n -> p n t"))
+
+        def quantise_qk(b, side):
+            nc.vector.quantize_mx(
+                out=qk_codes[:, b, side, :].bitcast(FP8X4),
+                scales=qk_planes[:, b, side, :],
+                in_=qk_grouped[:, b, side].rearrange("p n t -> p (n t)"),
+            )
+
+        bias = keep.tile([P, NODE_BLOCKS, N], BF16)
+
+        def make_bias():
+            for j in range(NODE_BLOCKS):
+                diagonal = m_sb[:, j, j * P : (j + 1) * P]
+                nc.gpsimd.affine_select(
+                    out=diagonal,
+                    in_=diagonal,
+                    compare_op=ALU.not_equal,
+                    fill=0.0,
+                    base=0,
+                    pattern=[[-1, P]],
+                    channel_multiplier=1,
+                )
+            nc.vector.tensor_scalar(
+                out=bias[:], in0=m_sb[:], scalar1=0.0, scalar2=EXCLUDED, op0=ALU.is_le, op1=ALU.mult
+            )
+            nc.vector.tensor_tensor(out=bias[:], in0=bias[:], in1=a_sb[:], op=ALU.add)
+
+        def attend(b, j):
+            nodes = slice(j * P, (j + 1) * P)
+            score = psum_score.tile([P, N], F32)
+            for first, (still, moving) in enumerate(((Q_SIDE, K_SIDE), (K_SIDE, Q_SIDE))):
+                nc.tensor.matmul_mx(
+                    out=score[:],
+                    lhsT=qk_codes[:, b, still, nodes].bitcast(FP8X4),
+                    lhsT_scale=qk_planes[:, b, still, nodes],
+                    rhs=qk_codes[:, b, moving, :].bitcast(FP8X4),
+                    rhs_scale=qk_planes[:, b, moving, :],
+                    start=(first == 0),
+                    stop=(first == 1),
+                )
+            logits = rows.tile([P, N], F32)
+            nc.vector.scalar_tensor_tensor(
+                out=logits[:], in0=score[:], scalar=HALF_SCALE, in1=bias[:, j, :], op0=ALU.mult, op1=ALU.add
+            )
+            neg_max = stats.tile([P, 1], F32)
+            nc.vector.tensor_reduce(out=neg_max[:], in_=logits[:], axis=AXIS.X, op=ALU.max, negate=True)
+            weights = rows.tile([P, N], F32)
+            row_sum = stats.tile([P, 1], F32)
+            nc.scalar.activation(
+                out=weights[:], in_=logits[:], func=ACT.Exp, bias=neg_max[:], scale=1.0, accum_out=row_sum[:]
+            )
+            inv_sum = stats.tile([P, 1], F32)
+            nc.vector.reciprocal(out=inv_sum[:], in_=row_sum[:])
+            nc.gpsimd.tensor_scalar(
+                out=weights[:], in0=weights[:], scalar1=inv_sum[:], scalar2=0.0, op0=ALU.mult, op1=ALU.add
+            )
+            nc.sync.dma_start(out=out[b, nodes, :], in_=weights[:])
+
+        flip_and_quantise_h(0)
+        flip_and_quantise_h(1)
+        for side in (Q_SIDE, K_SIDE):
+            for j in range(NODE_BLOCKS):
+                project(0, side, j, nc.scalar.copy if j % 2 == 0 else nc.vector.tensor_copy)
+            quantise_qk(0, side)
+        for side in (Q_SIDE, K_SIDE):
+            for j in range(NODE_BLOCKS):
+                project(1, side, j, nc.scalar.copy)
+        make_bias()
+        for j in range(NODE_BLOCKS):
+            attend(0, j)
+        for side in (Q_SIDE, K_SIDE):
+            quantise_qk(1, side)
+        for j in range(NODE_BLOCKS):
+            attend(1, j)

@@ -22,6 +22,9 @@ TAU = 1.5
 HALF_SCALE = 0.5 / (math.sqrt(C) * TAU)
 EXCLUDED = -1.0e30
 Q_SIDE, K_SIDE = 0, 1
+PAIRS = 4
+LAG = 1
+PAIRS_AHEAD = 2
 
 FLOPS = 2 * B * N * C * (2 * D) + 2 * B * N * N * D
 
@@ -32,11 +35,12 @@ def tile_dynamicgraphattention_kernel(
     nc = tc.nc
     with ExitStack() as ctx:
         keep = ctx.enter_context(tc.tile_pool(name="keep", bufs=1))
-        rows = ctx.enter_context(tc.tile_pool(name="rows", bufs=4))
-        stats = ctx.enter_context(tc.tile_pool(name="stats", bufs=4))
+        rows = ctx.enter_context(tc.tile_pool(name="rows", bufs=B * NODE_BLOCKS))
+        stats = ctx.enter_context(tc.tile_pool(name="stats", bufs=B * NODE_BLOCKS))
         psum_flip = ctx.enter_context(tc.psum_pool(name="psum_flip", bufs=2))
         psum_proj = ctx.enter_context(tc.psum_pool(name="psum_proj", bufs=4))
         psum_score = ctx.enter_context(tc.psum_pool(name="psum_score", bufs=2))
+        ctx.enter_context(tc.manual_schedule())
 
         identity = keep.tile([P, P], F32)
         make_identity(nc, identity[:])
@@ -80,29 +84,32 @@ def tile_dynamicgraphattention_kernel(
         h_codes = keep.tile([P, B, N], U32, align_bytes=64)
         h_plane = keep.tile([P, B, N], U8, align_bytes=64)
 
-        def flip_and_quantise_h(b):
-            for half in range(2):
-                flipped = psum_flip.tile([P, 2, 2 * P], F32)
-                for jj in range(2):
-                    words = h_sb[:, b, 2 * half + jj, :].bitcast(F32)
-                    for u in range(2):
-                        nc.tensor.transpose(
-                            flipped[:, u, jj * P : (jj + 1) * P], words[:, u : C // 2 : 2], identity[:]
-                        )
-                nodes = slice(2 * P * half, 2 * P * (half + 1))
-                copy = nc.vector.tensor_copy if half == 0 else nc.scalar.copy
-                copy(out=h_pairs[:, b, nodes, :], in_=flipped[:].rearrange("p u n -> p n u"))
+        def flip_h(b, half):
+            flipped = psum_flip.tile([P, 2, 2 * P], F32)
+            for jj in range(2):
+                words = h_sb[:, b, 2 * half + jj, :].bitcast(F32)
+                for u in range(2):
+                    nc.tensor.transpose(
+                        flipped[:, u, jj * P : (jj + 1) * P], words[:, u : C // 2 : 2], identity[:]
+                    )
+            nodes = slice(2 * P * half, 2 * P * (half + 1))
+            copy = nc.vector.tensor_copy if half == 0 else nc.scalar.copy
+            copy(out=h_pairs[:, b, nodes, :], in_=flipped[:].rearrange("p u n -> p n u"))
+
+        def quantise_h(b, half):
+            nodes = slice(2 * P * half, 2 * P * (half + 1))
             nc.vector.quantize_mx(
-                out=h_codes[:, b, :].bitcast(FP8X4),
-                scales=h_plane[:, b, :],
-                in_=h_pairs[:, b].rearrange("p n u -> p (n u)").bitcast(BF16),
+                out=h_codes[:, b, nodes].bitcast(FP8X4),
+                scales=h_plane[:, b, nodes],
+                in_=h_pairs[:, b, nodes, :].rearrange("p n u -> p (n u)").bitcast(BF16),
             )
 
         qk_grouped = keep.tile([P, B, 2, N, PACK], BF16, align_bytes=64)
         qk_codes = keep.tile([P, B, 2, N], U32, align_bytes=64)
         qk_planes = keep.tile([P, B, 2, N], U8, align_bytes=64)
 
-        def project(b, side, j, copy):
+        def project(b, bank, copy):
+            side, j = divmod(bank, NODE_BLOCKS)
             nodes = slice(j * P, (j + 1) * P)
             acc = psum_proj.tile([P, PACK, P], F32)
             for t in range(PACK):
@@ -118,33 +125,43 @@ def tile_dynamicgraphattention_kernel(
                 )
             copy(out=qk_grouped[:, b, side, nodes, :], in_=acc[:].rearrange("p t n -> p n t"))
 
-        def quantise_qk(b, side):
+        def project_pair_on_scalar(b, pair):
+            project(b, 2 * pair, nc.scalar.copy)
+            project(b, 2 * pair + 1, nc.scalar.copy)
+
+        def quantise_pair(b, pair):
+            side, half = divmod(pair, 2)
+            nodes = slice(2 * P * half, 2 * P * (half + 1))
             nc.vector.quantize_mx(
-                out=qk_codes[:, b, side, :].bitcast(FP8X4),
-                scales=qk_planes[:, b, side, :],
-                in_=qk_grouped[:, b, side].rearrange("p n t -> p (n t)"),
+                out=qk_codes[:, b, side, nodes].bitcast(FP8X4),
+                scales=qk_planes[:, b, side, nodes],
+                in_=qk_grouped[:, b, side, nodes, :].rearrange("p n t -> p (n t)"),
             )
 
         bias = keep.tile([P, NODE_BLOCKS, N], BF16)
 
-        def make_bias():
+        def penalise_excluded():
+            nc.vector.tensor_scalar(
+                out=bias[:], in0=m_sb[:], scalar1=0.0, scalar2=EXCLUDED, op0=ALU.is_le, op1=ALU.mult
+            )
+
+        def add_a_stat():
             for j in range(NODE_BLOCKS):
-                diagonal = m_sb[:, j, j * P : (j + 1) * P]
+                diagonal = a_sb[:, j, j * P : (j + 1) * P]
                 nc.gpsimd.affine_select(
                     out=diagonal,
                     in_=diagonal,
                     compare_op=ALU.not_equal,
-                    fill=0.0,
+                    fill=EXCLUDED,
                     base=0,
                     pattern=[[-1, P]],
                     channel_multiplier=1,
                 )
-            nc.vector.tensor_scalar(
-                out=bias[:], in0=m_sb[:], scalar1=0.0, scalar2=EXCLUDED, op0=ALU.is_le, op1=ALU.mult
-            )
             nc.vector.tensor_tensor(out=bias[:], in0=bias[:], in1=a_sb[:], op=ALU.add)
 
-        def attend(b, j):
+        logits, neg_max, weights, row_sum = {}, {}, {}, {}
+
+        def logits_and_max(i, b, j):
             nodes = slice(j * P, (j + 1) * P)
             score = psum_score.tile([P, N], F32)
             for first, (still, moving) in enumerate(((Q_SIDE, K_SIDE), (K_SIDE, Q_SIDE))):
@@ -157,37 +174,60 @@ def tile_dynamicgraphattention_kernel(
                     start=(first == 0),
                     stop=(first == 1),
                 )
-            logits = rows.tile([P, N], F32)
+            logits[i] = rows.tile([P, N], F32, name="logits")
             nc.vector.scalar_tensor_tensor(
-                out=logits[:], in0=score[:], scalar=HALF_SCALE, in1=bias[:, j, :], op0=ALU.mult, op1=ALU.add
+                out=logits[i][:], in0=score[:], scalar=HALF_SCALE, in1=bias[:, j, :], op0=ALU.mult, op1=ALU.add
             )
-            neg_max = stats.tile([P, 1], F32)
-            nc.vector.tensor_reduce(out=neg_max[:], in_=logits[:], axis=AXIS.X, op=ALU.max, negate=True)
-            weights = rows.tile([P, N], F32)
-            row_sum = stats.tile([P, 1], F32)
-            nc.scalar.activation(
-                out=weights[:], in_=logits[:], func=ACT.Exp, bias=neg_max[:], scale=1.0, accum_out=row_sum[:]
-            )
-            inv_sum = stats.tile([P, 1], F32)
-            nc.vector.reciprocal(out=inv_sum[:], in_=row_sum[:])
-            nc.gpsimd.tensor_scalar(
-                out=weights[:], in0=weights[:], scalar1=inv_sum[:], scalar2=0.0, op0=ALU.mult, op1=ALU.add
-            )
-            nc.sync.dma_start(out=out[b, nodes, :], in_=weights[:])
+            neg_max[i] = stats.tile([P, 1], F32, name="neg_max")
+            nc.vector.tensor_reduce(out=neg_max[i][:], in_=logits[i][:], axis=AXIS.X, op=ALU.max, negate=True)
 
-        flip_and_quantise_h(0)
-        flip_and_quantise_h(1)
-        for side in (Q_SIDE, K_SIDE):
-            for j in range(NODE_BLOCKS):
-                project(0, side, j, nc.scalar.copy if j % 2 == 0 else nc.vector.tensor_copy)
-            quantise_qk(0, side)
-        for side in (Q_SIDE, K_SIDE):
-            for j in range(NODE_BLOCKS):
-                project(1, side, j, nc.scalar.copy)
-        make_bias()
-        for j in range(NODE_BLOCKS):
-            attend(0, j)
-        for side in (Q_SIDE, K_SIDE):
-            quantise_qk(1, side)
-        for j in range(NODE_BLOCKS):
-            attend(1, j)
+        def exponentials(i):
+            weights[i] = rows.tile([P, N], F32, name="weights")
+            row_sum[i] = stats.tile([P, 1], F32, name="row_sum")
+            nc.scalar.activation(
+                out=weights[i][:],
+                in_=logits[i][:],
+                func=ACT.Exp,
+                bias=neg_max[i][:],
+                scale=1.0,
+                accum_out=row_sum[i][:],
+            )
+
+        def normalise_and_store(i):
+            b, j = divmod(i, NODE_BLOCKS)
+            inv_sum = stats.tile([P, 1], F32)
+            nc.vector.reciprocal(out=inv_sum[:], in_=row_sum[i][:])
+            nc.gpsimd.tensor_scalar(
+                out=weights[i][:], in0=weights[i][:], scalar1=inv_sum[:], scalar2=0.0, op0=ALU.mult, op1=ALU.add
+            )
+            nc.sync.dma_start(out=out[b, j * P : (j + 1) * P, :], in_=weights[i][:])
+
+        for b in range(B):
+            for half in range(2):
+                flip_h(b, half)
+            for half in range(2):
+                quantise_h(b, half)
+        for pair in range(PAIRS):
+            if pair == PAIRS - 1:
+                penalise_excluded()
+            project(0, 2 * pair, nc.scalar.copy)
+            project(0, 2 * pair + 1, nc.scalar.copy if pair % 2 == 0 else nc.vector.tensor_copy)
+            if pair > 0:
+                quantise_pair(0, pair - 1)
+        quantise_pair(0, PAIRS - 1)
+        add_a_stat()
+        for pair in range(PAIRS_AHEAD):
+            project_pair_on_scalar(1, pair)
+        for i in range(B * NODE_BLOCKS):
+            b, j = divmod(i, NODE_BLOCKS)
+            logits_and_max(i, b, j)
+            if i >= LAG:
+                normalise_and_store(i - LAG)
+            if PAIRS_AHEAD + i < PAIRS:
+                project_pair_on_scalar(1, PAIRS_AHEAD + i)
+            exponentials(i)
+            if i in (1, 2):
+                quantise_pair(1, 2 * i - 2)
+                quantise_pair(1, 2 * i - 1)
+        for i in range(B * NODE_BLOCKS - LAG, B * NODE_BLOCKS):
+            normalise_and_store(i)

@@ -22,9 +22,11 @@ TAU = 1.5
 HALF_SCALE = 0.5 / (math.sqrt(C) * TAU)
 EXCLUDED = -1.0e30
 Q_SIDE, K_SIDE = 0, 1
+ROW_BLOCKS = B * NODE_BLOCKS
+PSUM_BANKS = 8
+LAST_ON_VECTOR = 2
 PAIRS = 4
-LAG = 1
-PAIRS_AHEAD = 2
+PAIRS_AHEAD = 3
 
 FLOPS = 2 * B * N * C * (2 * D) + 2 * B * N * N * D
 
@@ -35,11 +37,9 @@ def tile_dynamicgraphattention_kernel(
     nc = tc.nc
     with ExitStack() as ctx:
         keep = ctx.enter_context(tc.tile_pool(name="keep", bufs=1))
-        rows = ctx.enter_context(tc.tile_pool(name="rows", bufs=B * NODE_BLOCKS))
-        stats = ctx.enter_context(tc.tile_pool(name="stats", bufs=B * NODE_BLOCKS))
-        psum_flip = ctx.enter_context(tc.psum_pool(name="psum_flip", bufs=2))
-        psum_proj = ctx.enter_context(tc.psum_pool(name="psum_proj", bufs=4))
-        psum_score = ctx.enter_context(tc.psum_pool(name="psum_score", bufs=2))
+        rows = ctx.enter_context(tc.tile_pool(name="rows", bufs=ROW_BLOCKS))
+        stats = ctx.enter_context(tc.tile_pool(name="stats", bufs=ROW_BLOCKS))
+        psum = ctx.enter_context(tc.psum_pool(name="psum", bufs=PSUM_BANKS))
         ctx.enter_context(tc.manual_schedule())
 
         identity = keep.tile([P, P], F32)
@@ -56,7 +56,10 @@ def tile_dynamicgraphattention_kernel(
         a_sb = keep.tile([P, NODE_BLOCKS, N], BF16)
 
         def load_h(b):
-            nc.sync.dma_start(out=h_sb[:, b], in_=H_t[b].rearrange("(j p) c -> p j c", p=P))
+            by_block = H_t[b].rearrange("(j p) c -> p j c", p=P)
+            for half in range(2):
+                blocks = slice(2 * half, 2 * half + 2)
+                nc.sync.dma_start(out=h_sb[:, b, blocks, :], in_=by_block[:, blocks, :])
 
         def load_scales(side, scales):
             by_r = scales[0].rearrange("(Q r) n -> r Q n", r=4)
@@ -85,7 +88,7 @@ def tile_dynamicgraphattention_kernel(
         h_plane = keep.tile([P, B, N], U8, align_bytes=64)
 
         def flip_h(b, half):
-            flipped = psum_flip.tile([P, 2, 2 * P], F32)
+            flipped = psum.tile([P, 2, 2 * P], F32, tag="bank")
             for jj in range(2):
                 words = h_sb[:, b, 2 * half + jj, :].bitcast(F32)
                 for u in range(2):
@@ -108,10 +111,9 @@ def tile_dynamicgraphattention_kernel(
         qk_codes = keep.tile([P, B, 2, N], U32, align_bytes=64)
         qk_planes = keep.tile([P, B, 2, N], U8, align_bytes=64)
 
-        def project(b, bank, copy):
-            side, j = divmod(bank, NODE_BLOCKS)
+        def project(b, side, j):
             nodes = slice(j * P, (j + 1) * P)
-            acc = psum_proj.tile([P, PACK, P], F32)
+            acc = psum.tile([P, PACK, P], F32, tag="bank")
             for t in range(PACK):
                 features = slice(t * P, (t + 1) * P)
                 nc.tensor.matmul_mx(
@@ -123,11 +125,13 @@ def tile_dynamicgraphattention_kernel(
                     start=True,
                     stop=True,
                 )
+            copy = nc.vector.tensor_copy if j == 1 else nc.scalar.copy
             copy(out=qk_grouped[:, b, side, nodes, :], in_=acc[:].rearrange("p t n -> p n t"))
 
-        def project_pair_on_scalar(b, pair):
-            project(b, 2 * pair, nc.scalar.copy)
-            project(b, 2 * pair + 1, nc.scalar.copy)
+        def project_pair(b, pair):
+            side, half = divmod(pair, 2)
+            project(b, side, 2 * half)
+            project(b, side, 2 * half + 1)
 
         def quantise_pair(b, pair):
             side, half = divmod(pair, 2)
@@ -157,13 +161,14 @@ def tile_dynamicgraphattention_kernel(
                     pattern=[[-1, P]],
                     channel_multiplier=1,
                 )
-            nc.vector.tensor_tensor(out=bias[:], in0=bias[:], in1=a_sb[:], op=ALU.add)
+                nc.gpsimd.tensor_tensor(out=bias[:, j, :], in0=bias[:, j, :], in1=a_sb[:, j, :], op=ALU.add)
 
         logits, neg_max, weights, row_sum = {}, {}, {}, {}
 
-        def logits_and_max(i, b, j):
+        def logits_and_max(i):
+            b, j = divmod(i, NODE_BLOCKS)
             nodes = slice(j * P, (j + 1) * P)
-            score = psum_score.tile([P, N], F32)
+            score = psum.tile([P, N], F32, tag="bank")
             for first, (still, moving) in enumerate(((Q_SIDE, K_SIDE), (K_SIDE, Q_SIDE))):
                 nc.tensor.matmul_mx(
                     out=score[:],
@@ -197,9 +202,12 @@ def tile_dynamicgraphattention_kernel(
             b, j = divmod(i, NODE_BLOCKS)
             inv_sum = stats.tile([P, 1], F32)
             nc.vector.reciprocal(out=inv_sum[:], in_=row_sum[i][:])
-            nc.gpsimd.tensor_scalar(
-                out=weights[i][:], in0=weights[i][:], scalar1=inv_sum[:], scalar2=0.0, op0=ALU.mult, op1=ALU.add
-            )
+            if i >= ROW_BLOCKS - LAST_ON_VECTOR:
+                nc.vector.tensor_scalar_mul(out=weights[i][:], in0=weights[i][:], scalar1=inv_sum[:])
+            else:
+                nc.gpsimd.tensor_scalar(
+                    out=weights[i][:], in0=weights[i][:], scalar1=inv_sum[:], scalar2=0.0, op0=ALU.mult, op1=ALU.add
+                )
             nc.sync.dma_start(out=out[b, j * P : (j + 1) * P, :], in_=weights[i][:])
 
         for b in range(B):
@@ -208,26 +216,25 @@ def tile_dynamicgraphattention_kernel(
             for half in range(2):
                 quantise_h(b, half)
         for pair in range(PAIRS):
-            if pair == PAIRS - 1:
-                penalise_excluded()
-            project(0, 2 * pair, nc.scalar.copy)
-            project(0, 2 * pair + 1, nc.scalar.copy if pair % 2 == 0 else nc.vector.tensor_copy)
+            project_pair(0, pair)
             if pair > 0:
                 quantise_pair(0, pair - 1)
+            if pair == 1:
+                penalise_excluded()
+                add_a_stat()
         quantise_pair(0, PAIRS - 1)
-        add_a_stat()
         for pair in range(PAIRS_AHEAD):
-            project_pair_on_scalar(1, pair)
-        for i in range(B * NODE_BLOCKS):
-            b, j = divmod(i, NODE_BLOCKS)
-            logits_and_max(i, b, j)
-            if i >= LAG:
-                normalise_and_store(i - LAG)
-            if PAIRS_AHEAD + i < PAIRS:
-                project_pair_on_scalar(1, PAIRS_AHEAD + i)
+            project_pair(1, pair)
+            if pair > 0:
+                quantise_pair(1, pair - 1)
+        for i in range(ROW_BLOCKS):
+            logits_and_max(i)
+            if i > 0:
+                normalise_and_store(i - 1)
+            pair = PAIRS_AHEAD + i
+            if pair < PAIRS:
+                project_pair(1, pair)
             exponentials(i)
-            if i in (1, 2):
-                quantise_pair(1, 2 * i - 2)
-                quantise_pair(1, 2 * i - 1)
-        for i in range(B * NODE_BLOCKS - LAG, B * NODE_BLOCKS):
-            normalise_and_store(i)
+            if pair <= PAIRS:
+                quantise_pair(1, pair - 1)
+        normalise_and_store(ROW_BLOCKS - 1)

import math
from contextlib import ExitStack

import concourse.mybir as mybir
from concourse.masks import make_identity

F32 = mybir.dt.float32
BF16 = mybir.dt.bfloat16
I32 = mybir.dt.int32
U32 = mybir.dt.uint32
U8 = mybir.dt.uint8
FP8X4 = mybir.dt.float8_e4m3fn_x4
ALU = mybir.AluOpType
ACT = mybir.ActivationFunctionType
AXIS = mybir.AxisListType

P = 128
PACK = 4
B, N, C, D = 2, 512, 512, 512
NODE_BLOCKS = N // P
TAU = 1.5
HALF_SCALE = 0.5 / (math.sqrt(C) * TAU)
EXCLUDED = -1.0e30
Q_SIDE, K_SIDE = 0, 1
ROW_BLOCKS = B * NODE_BLOCKS
PSUM_BANKS = 8
LAST_ON_VECTOR = 2
PAIRS = 4
PAIRS_AHEAD = 3

FLOPS = 2 * B * N * C * (2 * D) + 2 * B * N * N * D


def tile_dynamicgraphattention_kernel(
    tc, H_t, A_stat, M_mask, Wq_words, Wq_scales, Wk_words, Wk_scales, out
):
    nc = tc.nc
    with ExitStack() as ctx:
        keep = ctx.enter_context(tc.tile_pool(name="keep", bufs=1))
        rows = ctx.enter_context(tc.tile_pool(name="rows", bufs=ROW_BLOCKS))
        stats = ctx.enter_context(tc.tile_pool(name="stats", bufs=ROW_BLOCKS))
        psum = ctx.enter_context(tc.psum_pool(name="psum", bufs=PSUM_BANKS))
        ctx.enter_context(tc.manual_schedule())

        identity = keep.tile([P, P], F32)
        make_identity(nc, identity[:])
        w_planes = keep.tile([P, 2, D], U8, align_bytes=64)
        nc.vector.memset(w_planes[:].rearrange("p w n -> p (w n)").bitcast(I32), 0)
        warm = keep.tile([P, 1], F32)
        nc.vector.memset(warm[:], 0.0)
        nc.scalar.activation(out=warm[:], in_=warm[:], func=ACT.Exp)

        h_sb = keep.tile([P, B, NODE_BLOCKS, C], BF16)
        w_words = keep.tile([P, 2, D], U32, align_bytes=64)
        m_sb = keep.tile([P, NODE_BLOCKS, N], BF16)
        a_sb = keep.tile([P, NODE_BLOCKS, N], BF16)

        def load_h(b):
            by_block = H_t[b].rearrange("(j p) c -> p j c", p=P)
            for half in range(2):
                blocks = slice(2 * half, 2 * half + 2)
                nc.sync.dma_start(out=h_sb[:, b, blocks, :], in_=by_block[:, blocks, :])

        def load_scales(side, scales):
            by_r = scales[0].rearrange("(Q r) n -> r Q n", r=4)
            for r in range(4):
                nc.sync.dma_start(
                    out=w_planes[r:P:32, side, :].bitcast(I32), in_=by_r[r].bitcast(I32)
                )

        def load_words(side, words):
            nc.sync.dma_start(
                out=w_words[:, side, :].bitcast(I32),
                in_=words[0].rearrange("p n t -> p (n t)").bitcast(I32),
            )

        load_h(0)
        load_scales(Q_SIDE, Wq_scales)
        load_h(1)
        load_words(Q_SIDE, Wq_words)
        load_words(K_SIDE, Wk_words)
        load_scales(K_SIDE, Wk_scales)
        nc.sync.dma_start(out=m_sb[:], in_=M_mask.rearrange("(j p) m -> p j m", p=P))
        nc.sync.dma_start(out=a_sb[:], in_=A_stat.rearrange("(j p) m -> p j m", p=P))

        h_pairs = keep.tile([P, B, N, 2], F32, align_bytes=64)
        h_codes = keep.tile([P, B, N], U32, align_bytes=64)
        h_plane = keep.tile([P, B, N], U8, align_bytes=64)

        def flip_h(b, half):
            flipped = psum.tile([P, 2, 2 * P], F32, tag="bank")
            for jj in range(2):
                words = h_sb[:, b, 2 * half + jj, :].bitcast(F32)
                for u in range(2):
                    nc.tensor.transpose(
                        flipped[:, u, jj * P : (jj + 1) * P], words[:, u : C // 2 : 2], identity[:]
                    )
            nodes = slice(2 * P * half, 2 * P * (half + 1))
            copy = nc.vector.tensor_copy if half == 0 else nc.scalar.copy
            copy(out=h_pairs[:, b, nodes, :], in_=flipped[:].rearrange("p u n -> p n u"))

        def quantise_h(b, half):
            nodes = slice(2 * P * half, 2 * P * (half + 1))
            nc.vector.quantize_mx(
                out=h_codes[:, b, nodes].bitcast(FP8X4),
                scales=h_plane[:, b, nodes],
                in_=h_pairs[:, b, nodes, :].rearrange("p n u -> p (n u)").bitcast(BF16),
            )

        qk_grouped = keep.tile([P, B, 2, N, PACK], BF16, align_bytes=64)
        qk_codes = keep.tile([P, B, 2, N], U32, align_bytes=64)
        qk_planes = keep.tile([P, B, 2, N], U8, align_bytes=64)

        def project(b, side, j):
            nodes = slice(j * P, (j + 1) * P)
            acc = psum.tile([P, PACK, P], F32, tag="bank")
            for t in range(PACK):
                features = slice(t * P, (t + 1) * P)
                nc.tensor.matmul_mx(
                    out=acc[:, t, :],
                    lhsT=w_words[:, side, features].bitcast(FP8X4),
                    lhsT_scale=w_planes[:, side, features],
                    rhs=h_codes[:, b, nodes].bitcast(FP8X4),
                    rhs_scale=h_plane[:, b, nodes],
                    start=True,
                    stop=True,
                )
            copy = nc.vector.tensor_copy if j == 1 else nc.scalar.copy
            copy(out=qk_grouped[:, b, side, nodes, :], in_=acc[:].rearrange("p t n -> p n t"))

        def project_pair(b, pair):
            side, half = divmod(pair, 2)
            project(b, side, 2 * half)
            project(b, side, 2 * half + 1)

        def quantise_pair(b, pair):
            side, half = divmod(pair, 2)
            nodes = slice(2 * P * half, 2 * P * (half + 1))
            nc.vector.quantize_mx(
                out=qk_codes[:, b, side, nodes].bitcast(FP8X4),
                scales=qk_planes[:, b, side, nodes],
                in_=qk_grouped[:, b, side, nodes, :].rearrange("p n t -> p (n t)"),
            )

        bias = keep.tile([P, NODE_BLOCKS, N], BF16)

        def penalise_excluded():
            nc.vector.tensor_scalar(
                out=bias[:], in0=m_sb[:], scalar1=0.0, scalar2=EXCLUDED, op0=ALU.is_le, op1=ALU.mult
            )

        def add_a_stat():
            for j in range(NODE_BLOCKS):
                diagonal = a_sb[:, j, j * P : (j + 1) * P]
                nc.gpsimd.affine_select(
                    out=diagonal,
                    in_=diagonal,
                    compare_op=ALU.not_equal,
                    fill=EXCLUDED,
                    base=0,
                    pattern=[[-1, P]],
                    channel_multiplier=1,
                )
                nc.gpsimd.tensor_tensor(out=bias[:, j, :], in0=bias[:, j, :], in1=a_sb[:, j, :], op=ALU.add)

        logits, neg_max, weights, row_sum = {}, {}, {}, {}

        def logits_and_max(i):
            b, j = divmod(i, NODE_BLOCKS)
            nodes = slice(j * P, (j + 1) * P)
            score = psum.tile([P, N], F32, tag="bank")
            for first, (still, moving) in enumerate(((Q_SIDE, K_SIDE), (K_SIDE, Q_SIDE))):
                nc.tensor.matmul_mx(
                    out=score[:],
                    lhsT=qk_codes[:, b, still, nodes].bitcast(FP8X4),
                    lhsT_scale=qk_planes[:, b, still, nodes],
                    rhs=qk_codes[:, b, moving, :].bitcast(FP8X4),
                    rhs_scale=qk_planes[:, b, moving, :],
                    start=(first == 0),
                    stop=(first == 1),
                )
            logits[i] = rows.tile([P, N], F32, name="logits")
            nc.vector.scalar_tensor_tensor(
                out=logits[i][:], in0=score[:], scalar=HALF_SCALE, in1=bias[:, j, :], op0=ALU.mult, op1=ALU.add
            )
            neg_max[i] = stats.tile([P, 1], F32, name="neg_max")
            nc.vector.tensor_reduce(out=neg_max[i][:], in_=logits[i][:], axis=AXIS.X, op=ALU.max, negate=True)

        def exponentials(i):
            weights[i] = rows.tile([P, N], F32, name="weights")
            row_sum[i] = stats.tile([P, 1], F32, name="row_sum")
            nc.scalar.activation(
                out=weights[i][:],
                in_=logits[i][:],
                func=ACT.Exp,
                bias=neg_max[i][:],
                scale=1.0,
                accum_out=row_sum[i][:],
            )

        def normalise_and_store(i):
            b, j = divmod(i, NODE_BLOCKS)
            inv_sum = stats.tile([P, 1], F32)
            nc.vector.reciprocal(out=inv_sum[:], in_=row_sum[i][:])
            if i >= ROW_BLOCKS - LAST_ON_VECTOR:
                nc.vector.tensor_scalar_mul(out=weights[i][:], in0=weights[i][:], scalar1=inv_sum[:])
            else:
                nc.gpsimd.tensor_scalar(
                    out=weights[i][:], in0=weights[i][:], scalar1=inv_sum[:], scalar2=0.0, op0=ALU.mult, op1=ALU.add
                )
            nc.sync.dma_start(out=out[b, j * P : (j + 1) * P, :], in_=weights[i][:])

        for b in range(B):
            for half in range(2):
                flip_h(b, half)
            for half in range(2):
                quantise_h(b, half)
        for pair in range(PAIRS):
            project_pair(0, pair)
            if pair > 0:
                quantise_pair(0, pair - 1)
            if pair == 1:
                penalise_excluded()
                add_a_stat()
        quantise_pair(0, PAIRS - 1)
        for pair in range(PAIRS_AHEAD):
            project_pair(1, pair)
            if pair > 0:
                quantise_pair(1, pair - 1)
        for i in range(ROW_BLOCKS):
            logits_and_max(i)
            if i > 0:
                normalise_and_store(i - 1)
            pair = PAIRS_AHEAD + i
            if pair < PAIRS:
                project_pair(1, pair)
            exponentials(i)
            if pair <= PAIRS:
                quantise_pair(1, pair - 1)
        normalise_and_store(ROW_BLOCKS - 1)
